import numpy as np
import ml_dtypes


def mxq(x, axis, fmt="e4m3"):
    dtype, down = {"e4m3": (ml_dtypes.float8_e4m3fn, 7), "e5m2": (ml_dtypes.float8_e5m2, 14)}[fmt]
    v = np.moveaxis(np.asarray(x, np.float32).astype(ml_dtypes.bfloat16).astype(np.float64), axis, -1)
    blocks = v.reshape(v.shape[:-1] + (-1, 32))
    amax = np.abs(blocks).max(-1, keepdims=True)
    byte = np.maximum(np.where(amax > 0, np.frexp(amax)[1] - 1 + 127, 0) - down, 1)
    scale = np.exp2(byte - 127.0)
    codes = (blocks / scale).astype(np.float32).astype(dtype).astype(np.float64)
    return np.moveaxis((codes * scale).reshape(v.shape), -1, axis)


WIDE = False


def mx_kscale(k):
    if not WIDE:
        return np.ones(k)
    levels = np.array([10, -10, 5, -5, 0])
    if k % 512:
        return np.exp2(np.random.permutation(np.resize(levels, k // 32))).repeat(32)
    a = np.empty((k // 512, 16))
    for p in range(k // 512):
        a[p, :8] = np.random.permutation(np.resize(levels, 8))
        for g in range(8):
            far = levels[np.abs(levels - a[p, g]) >= 10]
            a[p, g + 8] = far[np.random.randint(len(far))]
    return np.exp2(a.ravel()).repeat(32)


BF16 = ml_dtypes.bfloat16


def bf(x):
    return np.asarray(x, np.float32).astype(BF16)


def f64(x):
    return np.asarray(x).astype(np.float64)


B, S, H, A, NH = 4, 128, 1536, 1536, 12
HD = A // NH
LN_EPS = 1e-5


def setup_inputs():
    s = mx_kscale(A)
    return {"ctx_heads": bf(np.random.standard_normal((B, NH, S, HD)) * s.reshape(NH, 1, HD)),
            "Wo": bf(np.random.standard_normal((H, A)) / np.sqrt(A) / s),
            "bo": bf(np.random.standard_normal(H) * 0.3),
            "features": bf(np.random.standard_normal((B, S, H))),
            "ln_g": bf(1.0 + 0.1 * np.random.standard_normal(H)),
            "ln_b": bf(0.2 * np.random.standard_normal(H))}


def core(ctx_heads, Wo, bo, features, ln_g, ln_b):
    ctx = f64(ctx_heads).transpose(0, 2, 1, 3).reshape(B, S, A)
    p = (mxq(ctx, 2, "e4m3") @ mxq(f64(Wo), 1, "e4m3").T) + f64(bo)
    y = p + f64(features)
    mu = y.mean(-1, keepdims=True)
    var = y.var(-1, keepdims=True)
    return (y - mu) / np.sqrt(var + LN_EPS) * f64(ln_g) + f64(ln_b)


def e4m3fn_bytes(y):
    return np.clip(np.asarray(y, np.float64), -448.0, 448.0).astype(np.float32).astype(ml_dtypes.float8_e4m3fn).view(np.uint8)


Y_SCALE = 210.0


def reference(ctx_heads, Wo, bo, features, ln_g, ln_b):
    out = core(ctx_heads, Wo, bo, features, ln_g, ln_b)
    return out, e4m3fn_bytes(out * Y_SCALE)

@@ -1,0 +1,254 @@
+from contextlib import ExitStack
+
+import concourse.mybir as mybir
+from concourse.masks import make_identity
+
+FLOPS = 2 * 512 * 1536 * 1536
+
+F32 = mybir.dt.float32
+BF16 = mybir.dt.bfloat16
+U32 = mybir.dt.uint32
+U8 = mybir.dt.uint8
+FP8X4 = mybir.dt.float8_e4m3fn_x4
+FP8 = mybir.dt.float8_e4m3fn
+ALU = mybir.AluOpType
+ACT = mybir.ActivationFunctionType
+
+P = 128
+NB = 4
+NH = 12
+K = 1536
+H = 1536
+NPASS = 3
+CH = 512
+NCH = 3
+LN_EPS = 1e-5
+Y_SCALE = 210.0
+
+
+def tile_hierarchicalattention_pb_kernel(tc, ctx_heads, Wo, bo, features, ln_g, ln_b, out_0, out_1):
+    nc = tc.nc
+    with ExitStack() as es:
+        keep = es.enter_context(tc.tile_pool(name="keep", bufs=1))
+        grp_pool = es.enter_context(tc.tile_pool(name="grp", bufs=6))
+        work = es.enter_context(tc.tile_pool(name="work", bufs=2))
+        o8_pool = es.enter_context(tc.tile_pool(name="o8p", bufs=6))
+        ps = es.enter_context(tc.psum_pool(name="ps", bufs=5))
+        psk = es.enter_context(tc.psum_pool(name="psk", bufs=1))
+        es.enter_context(tc.manual_schedule())
+
+        x_sb = [keep.tile([P, K], BF16, name="x%d" % b) for b in range(NB)]
+        w_sb = [keep.tile([P, K], BF16, name="w%d" % r) for r in range(12)]
+        f_sb = [keep.tile([P, H], BF16, name="f%d" % b) for b in range(NB)]
+        fb = [keep.tile([P, H], F32, name="fb%d" % b) for b in range(NB)]
+        y = [keep.tile([P, H], F32, name="y%d" % b) for b in range(NB)]
+        xq = [keep.tile([P, NPASS * P], U32, name="xq%d" % b, align_bytes=64) for b in range(NB)]
+        xs = [keep.tile([P, NPASS * P], U8, name="xs%d" % b, align_bytes=64) for b in range(NB)]
+        wq = keep.tile([P, NPASS, H], U32, name="wq", align_bytes=64)
+        ws = keep.tile([P, NPASS, H], U8, name="ws", align_bytes=64)
+        vec3 = keep.tile([P, H], BF16, name="vec3")
+        bo_b = keep.tile([P, H], BF16, name="bo_b")
+        ident_f = keep.tile([P, P], F32, name="ident_f")
+        ident_b = keep.tile([P, P], BF16, name="ident_b")
+        eps_t = keep.tile([P, 1], F32, name="eps_t")
+        warm = keep.tile([P, 1], F32, name="warm")
+        sqj = keep.tile([P, H], F32, name="sqj")
+        sums = [keep.tile([P, NCH], F32, name="sums%d" % b) for b in range(NB)]
+        junk3 = [keep.tile([P, NCH], F32, name="junk3%d" % b) for b in range(NB)]
+        negmean = [keep.tile([P, 1], F32, name="negmean%d" % b) for b in range(NB)]
+        ssq = [keep.tile([P, 1], F32, name="ssq%d" % b) for b in range(NB)]
+        std = [keep.tile([P, 1], F32, name="std%d" % b) for b in range(NB)]
+        rstd = [keep.tile([P, 1], F32, name="rstd%d" % b) for b in range(NB)]
+        gb = [psk.tile([P, 1024], BF16, name="gb%d" % i) for i in range(3)]
+        g_ps = [gb[0][:, 0:512], gb[0][:, 512:1024], gb[1][:, 0:512]]
+        b_ps = [gb[1][:, 512:1024], gb[2][:, 0:512], gb[2][:, 512:1024]]
+
+        nc.vector.memset(eps_t[:], LN_EPS)
+        nc.vector.memset(vec3[:], 0.0)
+        nc.scalar.activation(out=warm[:], in_=eps_t[:], func=ACT.Sqrt)
+        make_identity(nc, ident_f[:])
+        make_identity(nc, ident_b[:])
+
+        def load_ctx(b):
+            nc.sync.dma_start(
+                out=x_sb[b][:].rearrange("p (h d) -> p h d", h=NH),
+                in_=ctx_heads[b].rearrange("h s d -> s h d"),
+            )
+
+        def load_w(r):
+            nc.sync.dma_start(out=w_sb[r][:], in_=Wo[r * P : (r + 1) * P, :])
+
+        def load_f(b):
+            nc.sync.dma_start(out=f_sb[b][:], in_=features[b])
+
+        load_ctx(0)
+        load_w(0)
+        load_w(1)
+        for j, v in enumerate((bo, ln_g, ln_b)):
+            nc.sync.dma_start(out=vec3[j : j + 1, :], in_=v.rearrange("(o n) -> o n", o=1))
+        load_w(2)
+        load_w(3)
+        load_f(0)
+        load_w(4)
+        load_w(5)
+        load_f(1)
+        load_w(6)
+        load_w(7)
+        load_f(2)
+        load_w(8)
+        load_w(9)
+        load_f(3)
+        load_w(10)
+        load_w(11)
+        load_ctx(1)
+        load_ctx(2)
+        load_ctx(3)
+
+        def transpose_words(dst, src, g, u):
+            words = src[:].bitcast(F32)
+            nc.tensor.transpose(dst, words[:, 256 * g + u : 256 * (g + 1) : 2], ident_f[:])
+
+        def evacuate(pt, ncol):
+            grp = grp_pool.tile([P, 1024], BF16, name="grp", tag="grp", align_bytes=64)
+            a = ncol // 256
+            nc.scalar.copy(
+                out=grp[:, 0 : 2 * ncol].bitcast(F32).rearrange("p (a r u) -> p a r u", a=a, u=2),
+                in_=pt[:, 0:ncol].rearrange("p (a u r) -> p a r u", a=a, u=2),
+            )
+            return grp
+
+        def t_ctx(b):
+            pa = ps.tile([P, CH], F32, name="wk", tag="wk")
+            for g in range(2):
+                for u in range(2):
+                    transpose_words(pa[:, (2 * g + u) * P : (2 * g + u + 1) * P], x_sb[b], g, u)
+            pb = ps.tile([P, CH], F32, name="wk", tag="wk")
+            for u in range(2):
+                transpose_words(pb[:, u * P : (u + 1) * P], x_sb[b], 2, u)
+            return evacuate(pa, 512), evacuate(pb, 256)
+
+        def q_ctx(b, grps):
+            nc.vector.quantize_mx(out=xq[b][:, 0:256].bitcast(FP8X4), scales=xs[b][:, 0:256], in_=grps[0][:])
+            nc.vector.quantize_mx(
+                out=xq[b][:, 256:384].bitcast(FP8X4), scales=xs[b][:, 256:384], in_=grps[1][:, 0:512]
+            )
+
+        def pair(i):
+            grps = []
+            for g in range(NPASS):
+                pt = ps.tile([P, CH], F32, name="wk", tag="wk")
+                for a in range(2):
+                    for u in range(2):
+                        transpose_words(pt[:, (2 * a + u) * P : (2 * a + u + 1) * P], w_sb[2 * i + a], g, u)
+                grps.append(evacuate(pt, 512))
+            for g in range(NPASS):
+                cols = slice(256 * i, 256 * (i + 1))
+                nc.vector.quantize_mx(out=wq[:, g, cols].bitcast(FP8X4), scales=ws[:, g, cols], in_=grps[g][:])
+
+        def bcast(j, n, dst):
+            nc.tensor.matmul(
+                out=dst,
+                lhsT=ident_b[:, j : j + 1].to_broadcast([P, P]),
+                rhs=vec3[:, n * CH : (n + 1) * CH],
+                start=True,
+                stop=True,
+            )
+
+        def mm(b, n):
+            acc = ps.tile([P, CH], F32, name="wk", tag="wk")
+            for g in range(NPASS):
+                nc.tensor.matmul_mx(
+                    out=acc[:],
+                    lhsT=xq[b][:, g * P : (g + 1) * P].bitcast(FP8X4),
+                    lhsT_scale=xs[b][:, g * P : (g + 1) * P],
+                    rhs=wq[:, g, n * CH : (n + 1) * CH].bitcast(FP8X4),
+                    rhs_scale=ws[:, g, n * CH : (n + 1) * CH],
+                    start=(g == 0),
+                    stop=(g == NPASS - 1),
+                )
+            return acc
+
+        def fbadd(b):
+            nc.vector.tensor_tensor(out=fb[b][:], in0=f_sb[b][:], in1=bo_b[:], op=ALU.add)
+
+        def yadd(b, n, acc):
+            sl = slice(n * CH, (n + 1) * CH)
+            nc.vector.scalar_tensor_tensor(
+                out=y[b][:, sl], in0=acc[:], scalar=1.0, in1=fb[b][:, sl],
+                op0=ALU.mult, op1=ALU.add, accum_out=sums[b][:, n : n + 1],
+            )
+
+        def mean(b):
+            nc.vector.tensor_scalar(
+                out=junk3[b][:], in0=sums[b][:], scalar1=-1.0 / H, scalar2=None,
+                op0=ALU.mult, op1=ALU.add, accum_out=negmean[b][:],
+            )
+
+        q_ctx(0, t_ctx(0))
+        pair(0)
+        bca = ps.tile([P, 1024], BF16, name="wk", tag="wk")
+        bcast(0, 0, bca[:, 0:512])
+        bcast(0, 1, bca[:, 512:1024])
+        bcb = ps.tile([P, 1024], BF16, name="wk", tag="wk")
+        bcast(0, 2, bcb[:, 0:512])
+        nc.scalar.copy(out=bo_b[:, 0:1024], in_=bca[:])
+        nc.scalar.copy(out=bo_b[:, 1024:1536], in_=bcb[:, 0:512])
+        pair(1)
+        for n in range(NCH):
+            bcast(1, n, g_ps[n])
+        fbadd(0)
+        pair(2)
+        yadd(0, 0, mm(0, 0))
+        fbadd(1)
+        pair(3)
+        for n in range(NCH):
+            bcast(2, n, b_ps[n])
+        fbadd(2)
+        pair(4)
+        yadd(0, 1, mm(0, 1))
+        fbadd(3)
+        pair(5)
+        grps = t_ctx(1)
+        acc = mm(0, 2)
+        q_ctx(1, grps)
+        yadd(0, 2, acc)
+        mean(0)
+
+        for b in range(NB):
+            nxt = b + 1
+            nc.scalar.activation(
+                out=sqj[:], in_=y[b][:], func=ACT.Square, bias=negmean[b][:], scale=1.0, accum_out=ssq[b][:]
+            )
+            if nxt < NB:
+                acc0 = mm(nxt, 0)
+            t = work.tile([P, H], F32, name="t", tag="t")
+            for n in range(NCH):
+                sl = slice(n * CH, (n + 1) * CH)
+                nc.vector.scalar_tensor_tensor(
+                    out=t[:, sl], in0=y[b][:, sl], scalar=negmean[b][:], in1=g_ps[n], op0=ALU.add, op1=ALU.mult
+                )
+            nc.scalar.activation(out=std[b][:], in_=ssq[b][:], func=ACT.Sqrt, bias=eps_t[:], scale=1.0 / H)
+            if nxt < NB:
+                acc1 = mm(nxt, 1)
+            if nxt + 1 < NB:
+                grps = t_ctx(nxt + 1)
+            if nxt < NB:
+                yadd(nxt, 0, acc0)
+            nc.vector.reciprocal(out=rstd[b][:], in_=std[b][:])
+            o = work.tile([P, H], F32, name="o", tag="o")
+            for n in range(NCH):
+                sl = slice(n * CH, (n + 1) * CH)
+                nc.vector.scalar_tensor_tensor(
+                    out=o[:, sl], in0=t[:, sl], scalar=rstd[b][:], in1=b_ps[n], op0=ALU.mult, op1=ALU.add
+                )
+                nc.sync.dma_start(out=out_0[b, :, sl], in_=o[:, sl])
+                o8 = o8_pool.tile([P, CH], FP8, name="o8", tag="o8")
+                nc.scalar.activation(out=o8[:], in_=o[:, sl], func=ACT.Copy, scale=Y_SCALE, saturate=False)
+                nc.sync.dma_start(out=out_1[b, :, sl], in_=o8[:].bitcast(U8))
+            if nxt < NB:
+                acc2 = mm(nxt, 2)
+                yadd(nxt, 1, acc1)
+                if nxt + 1 < NB:
+                    q_ctx(nxt + 1, grps)
+                yadd(nxt, 2, acc2)
+                mean(nxt)

@@ -25,6 +25,9 @@ NCH = 3
 LN_EPS = 1e-5
 Y_SCALE = 210.0
 
+GP_TILES = [0,1,2]
+GP_FB = [1,2,3]
+
 
 def tile_hierarchicalattention_pb_kernel(tc, ctx_heads, Wo, bo, features, ln_g, ln_b, out_0, out_1):
     nc = tc.nc
@@ -32,13 +35,14 @@ def tile_hierarchicalattention_pb_kernel(tc, ctx_heads, Wo, bo, features, ln_g, 
         keep = es.enter_context(tc.tile_pool(name="keep", bufs=1))
         grp_pool = es.enter_context(tc.tile_pool(name="grp", bufs=6))
         work = es.enter_context(tc.tile_pool(name="work", bufs=2))
+        o_pool = es.enter_context(tc.tile_pool(name="op", bufs=3))
         o8_pool = es.enter_context(tc.tile_pool(name="o8p", bufs=6))
         ps = es.enter_context(tc.psum_pool(name="ps", bufs=5))
         psk = es.enter_context(tc.psum_pool(name="psk", bufs=1))
         es.enter_context(tc.manual_schedule())
 
         x_sb = [keep.tile([P, K], BF16, name="x%d" % b) for b in range(NB)]
-        w_sb = [keep.tile([P, K], BF16, name="w%d" % r) for r in range(12)]
+        wp = [keep.tile([P, 2, K], BF16, name="wp%d" % i) for i in range(6)]
         f_sb = [keep.tile([P, H], BF16, name="f%d" % b) for b in range(NB)]
         fb = [keep.tile([P, H], F32, name="fb%d" % b) for b in range(NB)]
         y = [keep.tile([P, H], F32, name="y%d" % b) for b in range(NB)]
@@ -46,8 +50,11 @@ def tile_hierarchicalattention_pb_kernel(tc, ctx_heads, Wo, bo, features, ln_g, 
         xs = [keep.tile([P, NPASS * P], U8, name="xs%d" % b, align_bytes=64) for b in range(NB)]
         wq = keep.tile([P, NPASS, H], U32, name="wq", align_bytes=64)
         ws = keep.tile([P, NPASS, H], U8, name="ws", align_bytes=64)
-        vec3 = keep.tile([P, H], BF16, name="vec3")
+        vbo = keep.tile([P, H], BF16, name="vbo")
+        vgb = keep.tile([P, H], BF16, name="vgb")
         bo_b = keep.tile([P, H], BF16, name="bo_b")
+        g_sb = keep.tile([P, CH], BF16, name="g_sb")
+        b_sb = keep.tile([P, CH], BF16, name="b_sb")
         ident_f = keep.tile([P, P], F32, name="ident_f")
         ident_b = keep.tile([P, P], BF16, name="ident_b")
         eps_t = keep.tile([P, 1], F32, name="eps_t")
@@ -63,11 +70,12 @@ def tile_hierarchicalattention_pb_kernel(tc, ctx_heads, Wo, bo, features, ln_g, 
         g_ps = [gb[0][:, 0:512], gb[0][:, 512:1024], gb[1][:, 0:512]]
         b_ps = [gb[1][:, 512:1024], gb[2][:, 0:512], gb[2][:, 512:1024]]
 
+        nc.vector.memset(vbo[:], 0.0)
         nc.vector.memset(eps_t[:], LN_EPS)
-        nc.vector.memset(vec3[:], 0.0)
-        nc.scalar.activation(out=warm[:], in_=eps_t[:], func=ACT.Sqrt)
-        make_identity(nc, ident_f[:])
         make_identity(nc, ident_b[:])
+        make_identity(nc, ident_f[:])
+        nc.gpsimd.memset(vgb[:], 0.0)
+        nc.scalar.activation(out=warm[:], in_=eps_t[:], func=ACT.Sqrt)
 
         def load_ctx(b):
             nc.sync.dma_start(
@@ -75,37 +83,30 @@ def tile_hierarchicalattention_pb_kernel(tc, ctx_heads, Wo, bo, features, ln_g, 
                 in_=ctx_heads[b].rearrange("h s d -> s h d"),
             )
 
-        def load_w(r):
-            nc.sync.dma_start(out=w_sb[r][:], in_=Wo[r * P : (r + 1) * P, :])
+        def load_pair(i):
+            nc.sync.dma_start(out=wp[i][:], in_=Wo[2 * i * P : (2 * i + 2) * P, :].rearrange("(a p) k -> p a k", a=2))
 
         def load_f(b):
             nc.sync.dma_start(out=f_sb[b][:], in_=features[b])
 
         load_ctx(0)
-        load_w(0)
-        load_w(1)
-        for j, v in enumerate((bo, ln_g, ln_b)):
-            nc.sync.dma_start(out=vec3[j : j + 1, :], in_=v.rearrange("(o n) -> o n", o=1))
-        load_w(2)
-        load_w(3)
+        nc.sync.dma_start(out=vbo[0:1, :], in_=bo.rearrange("(o n) -> o n", o=1))
+        nc.sync.dma_start(out=wp[0][:, 0, :], in_=Wo[0:P, :])
+        nc.sync.dma_start(out=wp[0][:, 1, :], in_=Wo[P : 2 * P, :])
+        load_pair(1)
         load_f(0)
-        load_w(4)
-        load_w(5)
-        load_f(1)
-        load_w(6)
-        load_w(7)
-        load_f(2)
-        load_w(8)
-        load_w(9)
-        load_f(3)
-        load_w(10)
-        load_w(11)
-        load_ctx(1)
-        load_ctx(2)
-        load_ctx(3)
+        load_pair(2)
+        nc.sync.dma_start(out=vgb[0:1, :], in_=ln_g.rearrange("(o n) -> o n", o=1))
+        nc.sync.dma_start(out=vgb[1:2, :], in_=ln_b.rearrange("(o n) -> o n", o=1))
+        load_pair(3)
+        load_pair(4)
+        load_pair(5)
+        for b in range(1, NB):
+            load_ctx(b)
+            load_f(b)
 
         def transpose_words(dst, src, g, u):
-            words = src[:].bitcast(F32)
+            words = src.bitcast(F32)
             nc.tensor.transpose(dst, words[:, 256 * g + u : 256 * (g + 1) : 2], ident_f[:])
 
         def evacuate(pt, ncol):
@@ -121,10 +122,10 @@ def tile_hierarchicalattention_pb_kernel(tc, ctx_heads, Wo, bo, features, ln_g, 
             pa = ps.tile([P, CH], F32, name="wk", tag="wk")
             for g in range(2):
                 for u in range(2):
-                    transpose_words(pa[:, (2 * g + u) * P : (2 * g + u + 1) * P], x_sb[b], g, u)
+                    transpose_words(pa[:, (2 * g + u) * P : (2 * g + u + 1) * P], x_sb[b][:], g, u)
             pb = ps.tile([P, CH], F32, name="wk", tag="wk")
             for u in range(2):
-                transpose_words(pb[:, u * P : (u + 1) * P], x_sb[b], 2, u)
+                transpose_words(pb[:, u * P : (u + 1) * P], x_sb[b][:], 2, u)
             return evacuate(pa, 512), evacuate(pb, 256)
 
         def q_ctx(b, grps):
@@ -139,17 +140,17 @@ def tile_hierarchicalattention_pb_kernel(tc, ctx_heads, Wo, bo, features, ln_g, 
                 pt = ps.tile([P, CH], F32, name="wk", tag="wk")
                 for a in range(2):
                     for u in range(2):
-                        transpose_words(pt[:, (2 * a + u) * P : (2 * a + u + 1) * P], w_sb[2 * i + a], g, u)
+                        transpose_words(pt[:, (2 * a + u) * P : (2 * a + u + 1) * P], wp[i][:, a, :], g, u)
                 grps.append(evacuate(pt, 512))
             for g in range(NPASS):
                 cols = slice(256 * i, 256 * (i + 1))
                 nc.vector.quantize_mx(out=wq[:, g, cols].bitcast(FP8X4), scales=ws[:, g, cols], in_=grps[g][:])
 
-        def bcast(j, n, dst):
+        def bcast(src, j, n, dst):
             nc.tensor.matmul(
                 out=dst,
                 lhsT=ident_b[:, j : j + 1].to_broadcast([P, P]),
-                rhs=vec3[:, n * CH : (n + 1) * CH],
+                rhs=src[:, n * CH : (n + 1) * CH],
                 start=True,
                 stop=True,
             )
@@ -169,7 +170,12 @@ def tile_hierarchicalattention_pb_kernel(tc, ctx_heads, Wo, bo, features, ln_g, 
             return acc
 
         def fbadd(b):
-            nc.vector.tensor_tensor(out=fb[b][:], in0=f_sb[b][:], in1=bo_b[:], op=ALU.add)
+            if b in GP_FB:
+                for n in range(NCH):
+                    sl = slice(n * CH, (n + 1) * CH)
+                    nc.gpsimd.tensor_tensor(out=fb[b][:, sl], in0=f_sb[b][:, sl], in1=bo_b[:, sl], op=ALU.add)
+            else:
+                nc.vector.tensor_tensor(out=fb[b][:], in0=f_sb[b][:], in1=bo_b[:], op=ALU.add)
 
         def yadd(b, n, acc):
             sl = slice(n * CH, (n + 1) * CH)
@@ -184,45 +190,57 @@ def tile_hierarchicalattention_pb_kernel(tc, ctx_heads, Wo, bo, features, ln_g, 
                 op0=ALU.mult, op1=ALU.add, accum_out=negmean[b][:],
             )
 
-        q_ctx(0, t_ctx(0))
-        pair(0)
+        def finish(b, n, o):
+            sl = slice(n * CH, (n + 1) * CH)
+            nc.sync.dma_start(out=out_0[b, :, sl], in_=o[:, sl])
+            o8 = o8_pool.tile([P, CH], FP8, name="o8", tag="o8")
+            nc.scalar.activation(out=o8[:], in_=o[:, sl], func=ACT.Copy, scale=Y_SCALE, saturate=False)
+            nc.sync.dma_start(out=out_1[b, :, sl], in_=o8[:].bitcast(U8))
+
+        grps = t_ctx(0)
         bca = ps.tile([P, 1024], BF16, name="wk", tag="wk")
-        bcast(0, 0, bca[:, 0:512])
-        bcast(0, 1, bca[:, 512:1024])
+        bcast(vbo, 0, 0, bca[:, 0:512])
+        bcast(vbo, 0, 1, bca[:, 512:1024])
         bcb = ps.tile([P, 1024], BF16, name="wk", tag="wk")
-        bcast(0, 2, bcb[:, 0:512])
+        bcast(vbo, 0, 2, bcb[:, 0:512])
         nc.scalar.copy(out=bo_b[:, 0:1024], in_=bca[:])
         nc.scalar.copy(out=bo_b[:, 1024:1536], in_=bcb[:, 0:512])
+        q_ctx(0, grps)
+        pair(0)
         pair(1)
-        for n in range(NCH):
-            bcast(1, n, g_ps[n])
-        fbadd(0)
         pair(2)
+        fbadd(0)
         yadd(0, 0, mm(0, 0))
-        fbadd(1)
         pair(3)
-        for n in range(NCH):
-            bcast(2, n, b_ps[n])
-        fbadd(2)
         pair(4)
         yadd(0, 1, mm(0, 1))
-        fbadd(3)
         pair(5)
         grps = t_ctx(1)
         acc = mm(0, 2)
+        for n in range(NCH):
+            bcast(vgb, 0, n, g_ps[n])
+        for n in range(NCH):
+            bcast(vgb, 1, n, b_ps[n])
         q_ctx(1, grps)
+        fbadd(1)
+        fbadd(2)
         yadd(0, 2, acc)
         mean(0)
+        if GP_TILES:
+            nc.scalar.copy(out=g_sb[:], in_=g_ps[2])
+            nc.scalar.copy(out=b_sb[:], in_=b_ps[2])
 
+        late = []
         for b in range(NB):
             nxt = b + 1
+            nv = NCH - 1 if b in GP_TILES else NCH
             nc.scalar.activation(
                 out=sqj[:], in_=y[b][:], func=ACT.Square, bias=negmean[b][:], scale=1.0, accum_out=ssq[b][:]
             )
             if nxt < NB:
                 acc0 = mm(nxt, 0)
             t = work.tile([P, H], F32, name="t", tag="t")
-            for n in range(NCH):
+            for n in range(nv):
                 sl = slice(n * CH, (n + 1) * CH)
                 nc.vector.scalar_tensor_tensor(
                     out=t[:, sl], in0=y[b][:, sl], scalar=negmean[b][:], in1=g_ps[n], op0=ALU.add, op1=ALU.mult
@@ -232,19 +250,31 @@ def tile_hierarchicalattention_pb_kernel(tc, ctx_heads, Wo, bo, features, ln_g, 
                 acc1 = mm(nxt, 1)
             if nxt + 1 < NB:
                 grps = t_ctx(nxt + 1)
+            for item in late:
+                finish(item[0], NCH - 1, item[1])
+            late = []
             if nxt < NB:
                 yadd(nxt, 0, acc0)
             nc.vector.reciprocal(out=rstd[b][:], in_=std[b][:])
-            o = work.tile([P, H], F32, name="o", tag="o")
-            for n in range(NCH):
+            o = o_pool.tile([P, H], F32, name="o", tag="o")
+            if nv < NCH:
+                sl = slice(nv * CH, (nv + 1) * CH)
+                z1 = work.tile([P, CH], F32, name="z1", tag="z1")
+                nc.gpsimd.tensor_scalar(
+                    out=z1[:], in0=y[b][:, sl], scalar1=negmean[b][:], scalar2=rstd[b][:], op0=ALU.add, op1=ALU.mult
+                )
+                z2 = work.tile([P, CH], F32, name="z2", tag="z2")
+                nc.gpsimd.tensor_tensor(out=z2[:], in0=z1[:], in1=g_sb[:], op=ALU.mult)
+                nc.gpsimd.tensor_tensor(out=o[:, sl], in0=z2[:], in1=b_sb[:], op=ALU.add)
+                late.append((b, o))
+            if nxt + 2 < NB:
+                fbadd(nxt + 2)
+            for n in range(nv):
                 sl = slice(n * CH, (n + 1) * CH)
                 nc.vector.scalar_tensor_tensor(
                     out=o[:, sl], in0=t[:, sl], scalar=rstd[b][:], in1=b_ps[n], op0=ALU.mult, op1=ALU.add
                 )
-                nc.sync.dma_start(out=out_0[b, :, sl], in_=o[:, sl])
-                o8 = o8_pool.tile([P, CH], FP8, name="o8", tag="o8")
-                nc.scalar.activation(out=o8[:], in_=o[:, sl], func=ACT.Copy, scale=Y_SCALE, saturate=False)
-                nc.sync.dma_start(out=out_1[b, :, sl], in_=o8[:].bitcast(U8))
+                finish(b, n, o)
             if nxt < NB:
                 acc2 = mm(nxt, 2)
                 yadd(nxt, 1, acc1)
@@ -252,3 +282,5 @@ def tile_hierarchicalattention_pb_kernel(tc, ctx_heads, Wo, bo, features, ln_g, 
                     q_ctx(nxt + 1, grps)
                 yadd(nxt, 2, acc2)
                 mean(nxt)
+        for item in late:
+            finish(item[0], NCH - 1, item[1])

@@ -26,6 +26,7 @@ LN_EPS = 1e-5
 Y_SCALE = 210.0
 
 GP_TILES = [0,1,2]
+N_WARM = 4
 GP_FB = [1,2,3]
 
 
@@ -55,6 +56,7 @@ def tile_hierarchicalattention_pb_kernel(tc, ctx_heads, Wo, bo, features, ln_g, 
         bo_b = keep.tile([P, H], BF16, name="bo_b")
         g_sb = keep.tile([P, CH], BF16, name="g_sb")
         b_sb = keep.tile([P, CH], BF16, name="b_sb")
+        zeros = keep.tile([P, CH], BF16, name="zeros")
         ident_f = keep.tile([P, P], F32, name="ident_f")
         ident_b = keep.tile([P, P], BF16, name="ident_b")
         eps_t = keep.tile([P, 1], F32, name="eps_t")
@@ -70,11 +72,12 @@ def tile_hierarchicalattention_pb_kernel(tc, ctx_heads, Wo, bo, features, ln_g, 
         g_ps = [gb[0][:, 0:512], gb[0][:, 512:1024], gb[1][:, 0:512]]
         b_ps = [gb[1][:, 512:1024], gb[2][:, 0:512], gb[2][:, 512:1024]]
 
+        nc.vector.memset(zeros[:], 0.0)
         nc.vector.memset(vbo[:], 0.0)
         nc.vector.memset(eps_t[:], LN_EPS)
         make_identity(nc, ident_b[:])
-        make_identity(nc, ident_f[:])
         nc.gpsimd.memset(vgb[:], 0.0)
+        make_identity(nc, ident_f[:])
         nc.scalar.activation(out=warm[:], in_=eps_t[:], func=ACT.Sqrt)
 
         def load_ctx(b):
@@ -93,11 +96,11 @@ def tile_hierarchicalattention_pb_kernel(tc, ctx_heads, Wo, bo, features, ln_g, 
         nc.sync.dma_start(out=vbo[0:1, :], in_=bo.rearrange("(o n) -> o n", o=1))
         nc.sync.dma_start(out=wp[0][:, 0, :], in_=Wo[0:P, :])
         nc.sync.dma_start(out=wp[0][:, 1, :], in_=Wo[P : 2 * P, :])
+        nc.sync.dma_start(out=vgb[0:1, :], in_=ln_g.rearrange("(o n) -> o n", o=1))
+        nc.sync.dma_start(out=vgb[1:2, :], in_=ln_b.rearrange("(o n) -> o n", o=1))
         load_pair(1)
         load_f(0)
         load_pair(2)
-        nc.sync.dma_start(out=vgb[0:1, :], in_=ln_g.rearrange("(o n) -> o n", o=1))
-        nc.sync.dma_start(out=vgb[1:2, :], in_=ln_b.rearrange("(o n) -> o n", o=1))
         load_pair(3)
         load_pair(4)
         load_pair(5)
@@ -197,38 +200,42 @@ def tile_hierarchicalattention_pb_kernel(tc, ctx_heads, Wo, bo, features, ln_g, 
             nc.scalar.activation(out=o8[:], in_=o[:, sl], func=ACT.Copy, scale=Y_SCALE, saturate=False)
             nc.sync.dma_start(out=out_1[b, :, sl], in_=o8[:].bitcast(U8))
 
+        dummy = ps.tile([P, CH], F32, name="wk", tag="wk")
+        for i in range(N_WARM):
+            nc.tensor.matmul(out=dummy[:], lhsT=ident_b[:], rhs=zeros[:], start=True, stop=True)
         grps = t_ctx(0)
         bca = ps.tile([P, 1024], BF16, name="wk", tag="wk")
         bcast(vbo, 0, 0, bca[:, 0:512])
         bcast(vbo, 0, 1, bca[:, 512:1024])
-        bcb = ps.tile([P, 1024], BF16, name="wk", tag="wk")
-        bcast(vbo, 0, 2, bcb[:, 0:512])
         nc.scalar.copy(out=bo_b[:, 0:1024], in_=bca[:])
-        nc.scalar.copy(out=bo_b[:, 1024:1536], in_=bcb[:, 0:512])
         q_ctx(0, grps)
         pair(0)
+        bcb = ps.tile([P, 1024], BF16, name="wk", tag="wk")
+        bcast(vbo, 0, 2, bcb[:, 0:512])
+        bcast(vgb, 0, 0, g_ps[0])
+        nc.scalar.copy(out=bo_b[:, 1024:1536], in_=bcb[:, 0:512])
         pair(1)
+        bcast(vgb, 0, 1, g_ps[1])
+        bcast(vgb, 0, 2, g_ps[2])
         pair(2)
+        for n in range(NCH):
+            bcast(vgb, 1, n, b_ps[n])
         fbadd(0)
-        yadd(0, 0, mm(0, 0))
         pair(3)
+        if GP_TILES:
+            nc.scalar.copy(out=g_sb[:], in_=g_ps[2])
+            nc.scalar.copy(out=b_sb[:], in_=b_ps[2])
+        yadd(0, 0, mm(0, 0))
         pair(4)
         yadd(0, 1, mm(0, 1))
         pair(5)
         grps = t_ctx(1)
         acc = mm(0, 2)
-        for n in range(NCH):
-            bcast(vgb, 0, n, g_ps[n])
-        for n in range(NCH):
-            bcast(vgb, 1, n, b_ps[n])
         q_ctx(1, grps)
         fbadd(1)
         fbadd(2)
         yadd(0, 2, acc)
         mean(0)
-        if GP_TILES:
-            nc.scalar.copy(out=g_sb[:], in_=g_ps[2])
-            nc.scalar.copy(out=b_sb[:], in_=b_ps[2])
 
         late = []
         for b in range(NB):
@@ -250,9 +257,6 @@ def tile_hierarchicalattention_pb_kernel(tc, ctx_heads, Wo, bo, features, ln_g, 
                 acc1 = mm(nxt, 1)
             if nxt + 1 < NB:
                 grps = t_ctx(nxt + 1)
-            for item in late:
-                finish(item[0], NCH - 1, item[1])
-            late = []
             if nxt < NB:
                 yadd(nxt, 0, acc0)
             nc.vector.reciprocal(out=rstd[b][:], in_=std[b][:])
@@ -266,7 +270,9 @@ def tile_hierarchicalattention_pb_kernel(tc, ctx_heads, Wo, bo, features, ln_g, 
                 z2 = work.tile([P, CH], F32, name="z2", tag="z2")
                 nc.gpsimd.tensor_tensor(out=z2[:], in0=z1[:], in1=g_sb[:], op=ALU.mult)
                 nc.gpsimd.tensor_tensor(out=o[:, sl], in0=z2[:], in1=b_sb[:], op=ALU.add)
-                late.append((b, o))
+                fresh = [(b, o)]
+            else:
+                fresh = []
             if nxt + 2 < NB:
                 fbadd(nxt + 2)
             for n in range(nv):
@@ -275,6 +281,9 @@ def tile_hierarchicalattention_pb_kernel(tc, ctx_heads, Wo, bo, features, ln_g, 
                     out=o[:, sl], in0=t[:, sl], scalar=rstd[b][:], in1=b_ps[n], op0=ALU.mult, op1=ALU.add
                 )
                 finish(b, n, o)
+            for item in late:
+                finish(item[0], NCH - 1, item[1])
+            late = fresh
             if nxt < NB:
                 acc2 = mm(nxt, 2)
                 yadd(nxt, 1, acc1)

@@ -34,10 +34,12 @@ def tile_hierarchicalattention_pb_kernel(tc, ctx_heads, Wo, bo, features, ln_g, 
     nc = tc.nc
     with ExitStack() as es:
         keep = es.enter_context(tc.tile_pool(name="keep", bufs=1))
-        grp_pool = es.enter_context(tc.tile_pool(name="grp", bufs=6))
+        grp_pool = es.enter_context(tc.tile_pool(name="grp", bufs=5))
+        perm_pool = es.enter_context(tc.tile_pool(name="perm", bufs=3))
+        zpool = es.enter_context(tc.tile_pool(name="zp", bufs=1))
         work = es.enter_context(tc.tile_pool(name="work", bufs=2))
         o_pool = es.enter_context(tc.tile_pool(name="op", bufs=3))
-        o8_pool = es.enter_context(tc.tile_pool(name="o8p", bufs=6))
+        o8_pool = es.enter_context(tc.tile_pool(name="o8p", bufs=4))
         ps = es.enter_context(tc.psum_pool(name="ps", bufs=5))
         psk = es.enter_context(tc.psum_pool(name="psk", bufs=1))
         es.enter_context(tc.manual_schedule())
@@ -61,7 +63,7 @@ def tile_hierarchicalattention_pb_kernel(tc, ctx_heads, Wo, bo, features, ln_g, 
         ident_b = keep.tile([P, P], BF16, name="ident_b")
         eps_t = keep.tile([P, 1], F32, name="eps_t")
         warm = keep.tile([P, 1], F32, name="warm")
-        sqj = keep.tile([P, H], F32, name="sqj")
+        sqj = keep.tile([P, H], BF16, name="sqj")
         sums = [keep.tile([P, NCH], F32, name="sums%d" % b) for b in range(NB)]
         junk3 = [keep.tile([P, NCH], F32, name="junk3%d" % b) for b in range(NB)]
         negmean = [keep.tile([P, 1], F32, name="negmean%d" % b) for b in range(NB)]
@@ -103,14 +105,23 @@ def tile_hierarchicalattention_pb_kernel(tc, ctx_heads, Wo, bo, features, ln_g, 
         load_pair(2)
         load_pair(3)
         load_pair(4)
-        load_pair(5)
+        for g in range(NPASS):
+            nc.sync.dma_start(
+                out=wp[5][:, :, g * 512 : (g + 1) * 512],
+                in_=Wo[10 * P : 12 * P, g * 512 : (g + 1) * 512].rearrange("(a p) k -> p a k", a=2),
+            )
         for b in range(1, NB):
             load_ctx(b)
             load_f(b)
 
-        def transpose_words(dst, src, g, u):
-            words = src.bitcast(F32)
-            nc.tensor.transpose(dst, words[:, 256 * g + u : 256 * (g + 1) : 2], ident_f[:])
+        def transpose_words(dst, perm, c, u):
+            nc.tensor.transpose(dst, perm[:, (2 * c + u) * P : (2 * c + u + 1) * P], ident_f[:])
+
+        def permute(perm, c0, nstr, words):
+            nc.vector.tensor_copy(
+                out=perm[:, c0 * 256 : (c0 + nstr) * 256].rearrange("p (c u m) -> p c u m", c=nstr, u=2),
+                in_=words.rearrange("p (c m u) -> p c u m", c=nstr, u=2),
+            )
 
         def evacuate(pt, ncol):
             grp = grp_pool.tile([P, 1024], BF16, name="grp", tag="grp", align_bytes=64)
@@ -122,13 +133,16 @@ def tile_hierarchicalattention_pb_kernel(tc, ctx_heads, Wo, bo, features, ln_g, 
             return grp
 
         def t_ctx(b):
+            words = x_sb[b][:].bitcast(F32)
             pa = ps.tile([P, CH], F32, name="wk", tag="wk")
             for g in range(2):
                 for u in range(2):
-                    transpose_words(pa[:, (2 * g + u) * P : (2 * g + u + 1) * P], x_sb[b][:], g, u)
+                    nc.tensor.transpose(
+                        pa[:, (2 * g + u) * P : (2 * g + u + 1) * P], words[:, 256 * g + u : 256 * (g + 1) : 2], ident_f[:]
+                    )
             pb = ps.tile([P, CH], F32, name="wk", tag="wk")
             for u in range(2):
-                transpose_words(pb[:, u * P : (u + 1) * P], x_sb[b][:], 2, u)
+                nc.tensor.transpose(pb[:, u * P : (u + 1) * P], words[:, 512 + u : 768 : 2], ident_f[:])
             return evacuate(pa, 512), evacuate(pb, 256)
 
         def q_ctx(b, grps):
@@ -137,13 +151,23 @@ def tile_hierarchicalattention_pb_kernel(tc, ctx_heads, Wo, bo, features, ln_g, 
                 out=xq[b][:, 256:384].bitcast(FP8X4), scales=xs[b][:, 256:384], in_=grps[1][:, 0:512]
             )
 
-        def pair(i):
+        def permute_pair(i):
+            pm = perm_pool.tile([P, K], F32, name="pm", tag="pm")
+            if i < 5:
+                permute(pm, 0, 2 * NPASS, wp[i][:].rearrange("p a k -> p (a k)").bitcast(F32))
+            else:
+                for g in range(NPASS):
+                    for a in range(2):
+                        permute(pm, a * NPASS + g, 1, wp[i][:, a, g * 512 : (g + 1) * 512].bitcast(F32))
+            return pm
+
+        def pair(i, pm):
             grps = []
             for g in range(NPASS):
                 pt = ps.tile([P, CH], F32, name="wk", tag="wk")
                 for a in range(2):
                     for u in range(2):
-                        transpose_words(pt[:, (2 * a + u) * P : (2 * a + u + 1) * P], wp[i][:, a, :], g, u)
+                        transpose_words(pt[:, (2 * a + u) * P : (2 * a + u + 1) * P], pm, a * NPASS + g, u)
                 grps.append(evacuate(pt, 512))
             for g in range(NPASS):
                 cols = slice(256 * i, 256 * (i + 1))
@@ -193,42 +217,49 @@ def tile_hierarchicalattention_pb_kernel(tc, ctx_heads, Wo, bo, features, ln_g, 
                 op0=ALU.mult, op1=ALU.add, accum_out=negmean[b][:],
             )
 
-        def finish(b, n, o):
-            sl = slice(n * CH, (n + 1) * CH)
-            nc.sync.dma_start(out=out_0[b, :, sl], in_=o[:, sl])
+        def finish(b, lo, hi, o):
+            nc.sync.dma_start(out=out_0[b, :, lo:hi], in_=o[:, lo:hi])
             o8 = o8_pool.tile([P, CH], FP8, name="o8", tag="o8")
-            nc.scalar.activation(out=o8[:], in_=o[:, sl], func=ACT.Copy, scale=Y_SCALE, saturate=False)
-            nc.sync.dma_start(out=out_1[b, :, sl], in_=o8[:].bitcast(U8))
+            nc.scalar.activation(
+                out=o8[:, 0 : hi - lo], in_=o[:, lo:hi], func=ACT.Copy, scale=Y_SCALE, saturate=False
+            )
+            nc.sync.dma_start(out=out_1[b, :, lo:hi], in_=o8[:, 0 : hi - lo].bitcast(U8))
 
         dummy = ps.tile([P, CH], F32, name="wk", tag="wk")
         for i in range(N_WARM):
             nc.tensor.matmul(out=dummy[:], lhsT=ident_b[:], rhs=zeros[:], start=True, stop=True)
         grps = t_ctx(0)
+        pm0 = permute_pair(0)
         bca = ps.tile([P, 1024], BF16, name="wk", tag="wk")
         bcast(vbo, 0, 0, bca[:, 0:512])
         bcast(vbo, 0, 1, bca[:, 512:1024])
         nc.scalar.copy(out=bo_b[:, 0:1024], in_=bca[:])
         q_ctx(0, grps)
-        pair(0)
+        pm1 = permute_pair(1)
+        pair(0, pm0)
         bcb = ps.tile([P, 1024], BF16, name="wk", tag="wk")
         bcast(vbo, 0, 2, bcb[:, 0:512])
         bcast(vgb, 0, 0, g_ps[0])
         nc.scalar.copy(out=bo_b[:, 1024:1536], in_=bcb[:, 0:512])
-        pair(1)
+        pm2 = permute_pair(2)
+        pair(1, pm1)
         bcast(vgb, 0, 1, g_ps[1])
         bcast(vgb, 0, 2, g_ps[2])
-        pair(2)
+        pm3 = permute_pair(3)
+        pair(2, pm2)
         for n in range(NCH):
             bcast(vgb, 1, n, b_ps[n])
         fbadd(0)
-        pair(3)
+        pm4 = permute_pair(4)
+        pair(3, pm3)
         if GP_TILES:
             nc.scalar.copy(out=g_sb[:], in_=g_ps[2])
             nc.scalar.copy(out=b_sb[:], in_=b_ps[2])
         yadd(0, 0, mm(0, 0))
-        pair(4)
+        pm5 = permute_pair(5)
+        pair(4, pm4)
         yadd(0, 1, mm(0, 1))
-        pair(5)
+        pair(5, pm5)
         grps = t_ctx(1)
         acc = mm(0, 2)
         q_ctx(1, grps)
@@ -263,11 +294,11 @@ def tile_hierarchicalattention_pb_kernel(tc, ctx_heads, Wo, bo, features, ln_g, 
             o = o_pool.tile([P, H], F32, name="o", tag="o")
             if nv < NCH:
                 sl = slice(nv * CH, (nv + 1) * CH)
-                z1 = work.tile([P, CH], F32, name="z1", tag="z1")
+                z1 = zpool.tile([P, CH], F32, name="z1", tag="z1")
                 nc.gpsimd.tensor_scalar(
                     out=z1[:], in0=y[b][:, sl], scalar1=negmean[b][:], scalar2=rstd[b][:], op0=ALU.add, op1=ALU.mult
                 )
-                z2 = work.tile([P, CH], F32, name="z2", tag="z2")
+                z2 = zpool.tile([P, CH], F32, name="z2", tag="z2")
                 nc.gpsimd.tensor_tensor(out=z2[:], in0=z1[:], in1=g_sb[:], op=ALU.mult)
                 nc.gpsimd.tensor_tensor(out=o[:, sl], in0=z2[:], in1=b_sb[:], op=ALU.add)
                 fresh = [(b, o)]
@@ -276,14 +307,20 @@ def tile_hierarchicalattention_pb_kernel(tc, ctx_heads, Wo, bo, features, ln_g, 
             if nxt + 2 < NB:
                 fbadd(nxt + 2)
             for n in range(nv):
-                sl = slice(n * CH, (n + 1) * CH)
-                nc.vector.scalar_tensor_tensor(
-                    out=o[:, sl], in0=t[:, sl], scalar=rstd[b][:], in1=b_ps[n], op0=ALU.mult, op1=ALU.add
-                )
-                finish(b, n, o)
-            for item in late:
-                finish(item[0], NCH - 1, item[1])
-            late = fresh
+                halves = 2 if (b == NB - 1 and n == NCH - 1) else 1
+                w = CH // halves
+                for h in range(halves):
+                    lo = n * CH + h * w
+                    nc.vector.scalar_tensor_tensor(
+                        out=o[:, lo : lo + w], in0=t[:, lo : lo + w], scalar=rstd[b][:],
+                        in1=b_ps[n][:, h * w : (h + 1) * w], op0=ALU.mult, op1=ALU.add,
+                    )
+                    finish(b, lo, lo + w, o)
+                if n == 1:
+                    for item in late:
+                        finish(item[0], (NCH - 1) * CH, H, item[1])
+                    late = []
+            late = late + fresh
             if nxt < NB:
                 acc2 = mm(nxt, 2)
                 yadd(nxt, 1, acc1)
@@ -292,4 +329,4 @@ def tile_hierarchicalattention_pb_kernel(tc, ctx_heads, Wo, bo, features, ln_g, 
                 yadd(nxt, 2, acc2)
                 mean(nxt)
         for item in late:
-            finish(item[0], NCH - 1, item[1])
+            finish(item[0], (NCH - 1) * CH, H, item[1])

@@ -26,6 +26,7 @@ LN_EPS = 1e-5
 Y_SCALE = 210.0
 
 GP_TILES = [0,1,2]
+LATE_AFTER = [1, 1, 1, 1]
 N_WARM = 4
 GP_FB = [1,2,3]
 
@@ -34,12 +35,10 @@ def tile_hierarchicalattention_pb_kernel(tc, ctx_heads, Wo, bo, features, ln_g, 
     nc = tc.nc
     with ExitStack() as es:
         keep = es.enter_context(tc.tile_pool(name="keep", bufs=1))
-        grp_pool = es.enter_context(tc.tile_pool(name="grp", bufs=5))
-        perm_pool = es.enter_context(tc.tile_pool(name="perm", bufs=3))
-        zpool = es.enter_context(tc.tile_pool(name="zp", bufs=1))
+        grp_pool = es.enter_context(tc.tile_pool(name="grp", bufs=6))
         work = es.enter_context(tc.tile_pool(name="work", bufs=2))
         o_pool = es.enter_context(tc.tile_pool(name="op", bufs=3))
-        o8_pool = es.enter_context(tc.tile_pool(name="o8p", bufs=4))
+        o8_pool = es.enter_context(tc.tile_pool(name="o8p", bufs=6))
         ps = es.enter_context(tc.psum_pool(name="ps", bufs=5))
         psk = es.enter_context(tc.psum_pool(name="psk", bufs=1))
         es.enter_context(tc.manual_schedule())
@@ -63,13 +62,14 @@ def tile_hierarchicalattention_pb_kernel(tc, ctx_heads, Wo, bo, features, ln_g, 
         ident_b = keep.tile([P, P], BF16, name="ident_b")
         eps_t = keep.tile([P, 1], F32, name="eps_t")
         warm = keep.tile([P, 1], F32, name="warm")
-        sqj = keep.tile([P, H], BF16, name="sqj")
+        sqj = keep.tile([P, H], F32, name="sqj")
         sums = [keep.tile([P, NCH], F32, name="sums%d" % b) for b in range(NB)]
         junk3 = [keep.tile([P, NCH], F32, name="junk3%d" % b) for b in range(NB)]
         negmean = [keep.tile([P, 1], F32, name="negmean%d" % b) for b in range(NB)]
         ssq = [keep.tile([P, 1], F32, name="ssq%d" % b) for b in range(NB)]
         std = [keep.tile([P, 1], F32, name="std%d" % b) for b in range(NB)]
         rstd = [keep.tile([P, 1], F32, name="rstd%d" % b) for b in range(NB)]
+        nmr = [keep.tile([P, 1], F32, name="nmr%d" % b) for b in range(NB)]
         gb = [psk.tile([P, 1024], BF16, name="gb%d" % i) for i in range(3)]
         g_ps = [gb[0][:, 0:512], gb[0][:, 512:1024], gb[1][:, 0:512]]
         b_ps = [gb[1][:, 512:1024], gb[2][:, 0:512], gb[2][:, 512:1024]]
@@ -114,14 +114,9 @@ def tile_hierarchicalattention_pb_kernel(tc, ctx_heads, Wo, bo, features, ln_g, 
             load_ctx(b)
             load_f(b)
 
-        def transpose_words(dst, perm, c, u):
-            nc.tensor.transpose(dst, perm[:, (2 * c + u) * P : (2 * c + u + 1) * P], ident_f[:])
-
-        def permute(perm, c0, nstr, words):
-            nc.vector.tensor_copy(
-                out=perm[:, c0 * 256 : (c0 + nstr) * 256].rearrange("p (c u m) -> p c u m", c=nstr, u=2),
-                in_=words.rearrange("p (c m u) -> p c u m", c=nstr, u=2),
-            )
+        def transpose_words(dst, src, g, u):
+            words = src.bitcast(F32)
+            nc.tensor.transpose(dst, words[:, 256 * g + u : 256 * (g + 1) : 2], ident_f[:])
 
         def evacuate(pt, ncol):
             grp = grp_pool.tile([P, 1024], BF16, name="grp", tag="grp", align_bytes=64)
@@ -133,17 +128,17 @@ def tile_hierarchicalattention_pb_kernel(tc, ctx_heads, Wo, bo, features, ln_g, 
             return grp
 
         def t_ctx(b):
-            words = x_sb[b][:].bitcast(F32)
             pa = ps.tile([P, CH], F32, name="wk", tag="wk")
             for g in range(2):
                 for u in range(2):
-                    nc.tensor.transpose(
-                        pa[:, (2 * g + u) * P : (2 * g + u + 1) * P], words[:, 256 * g + u : 256 * (g + 1) : 2], ident_f[:]
-                    )
+                    transpose_words(pa[:, (2 * g + u) * P : (2 * g + u + 1) * P], x_sb[b][:], g, u)
             pb = ps.tile([P, CH], F32, name="wk", tag="wk")
             for u in range(2):
-                nc.tensor.transpose(pb[:, u * P : (u + 1) * P], words[:, 512 + u : 768 : 2], ident_f[:])
-            return evacuate(pa, 512), evacuate(pb, 256)
+                transpose_words(pb[:, u * P : (u + 1) * P], x_sb[b][:], 2, u)
+            return pa, pb
+
+        def e_ctx(pts):
+            return evacuate(pts[0], 512), evacuate(pts[1], 256)
 
         def q_ctx(b, grps):
             nc.vector.quantize_mx(out=xq[b][:, 0:256].bitcast(FP8X4), scales=xs[b][:, 0:256], in_=grps[0][:])
@@ -151,23 +146,13 @@ def tile_hierarchicalattention_pb_kernel(tc, ctx_heads, Wo, bo, features, ln_g, 
                 out=xq[b][:, 256:384].bitcast(FP8X4), scales=xs[b][:, 256:384], in_=grps[1][:, 0:512]
             )
 
-        def permute_pair(i):
-            pm = perm_pool.tile([P, K], F32, name="pm", tag="pm")
-            if i < 5:
-                permute(pm, 0, 2 * NPASS, wp[i][:].rearrange("p a k -> p (a k)").bitcast(F32))
-            else:
-                for g in range(NPASS):
-                    for a in range(2):
-                        permute(pm, a * NPASS + g, 1, wp[i][:, a, g * 512 : (g + 1) * 512].bitcast(F32))
-            return pm
-
-        def pair(i, pm):
+        def pair(i):
             grps = []
             for g in range(NPASS):
                 pt = ps.tile([P, CH], F32, name="wk", tag="wk")
                 for a in range(2):
                     for u in range(2):
-                        transpose_words(pt[:, (2 * a + u) * P : (2 * a + u + 1) * P], pm, a * NPASS + g, u)
+                        transpose_words(pt[:, (2 * a + u) * P : (2 * a + u + 1) * P], wp[i][:, a, :], g, u)
                 grps.append(evacuate(pt, 512))
             for g in range(NPASS):
                 cols = slice(256 * i, 256 * (i + 1))
@@ -228,105 +213,116 @@ def tile_hierarchicalattention_pb_kernel(tc, ctx_heads, Wo, bo, features, ln_g, 
         dummy = ps.tile([P, CH], F32, name="wk", tag="wk")
         for i in range(N_WARM):
             nc.tensor.matmul(out=dummy[:], lhsT=ident_b[:], rhs=zeros[:], start=True, stop=True)
-        grps = t_ctx(0)
-        pm0 = permute_pair(0)
+        grps = e_ctx(t_ctx(0))
         bca = ps.tile([P, 1024], BF16, name="wk", tag="wk")
         bcast(vbo, 0, 0, bca[:, 0:512])
         bcast(vbo, 0, 1, bca[:, 512:1024])
         nc.scalar.copy(out=bo_b[:, 0:1024], in_=bca[:])
         q_ctx(0, grps)
-        pm1 = permute_pair(1)
-        pair(0, pm0)
+        pair(0)
         bcb = ps.tile([P, 1024], BF16, name="wk", tag="wk")
         bcast(vbo, 0, 2, bcb[:, 0:512])
         bcast(vgb, 0, 0, g_ps[0])
         nc.scalar.copy(out=bo_b[:, 1024:1536], in_=bcb[:, 0:512])
-        pm2 = permute_pair(2)
-        pair(1, pm1)
+        pair(1)
         bcast(vgb, 0, 1, g_ps[1])
         bcast(vgb, 0, 2, g_ps[2])
-        pm3 = permute_pair(3)
-        pair(2, pm2)
+        pair(2)
         for n in range(NCH):
             bcast(vgb, 1, n, b_ps[n])
         fbadd(0)
-        pm4 = permute_pair(4)
-        pair(3, pm3)
+        pair(3)
         if GP_TILES:
             nc.scalar.copy(out=g_sb[:], in_=g_ps[2])
             nc.scalar.copy(out=b_sb[:], in_=b_ps[2])
         yadd(0, 0, mm(0, 0))
-        pm5 = permute_pair(5)
-        pair(4, pm4)
+        pair(4)
         yadd(0, 1, mm(0, 1))
-        pair(5, pm5)
-        grps = t_ctx(1)
-        acc = mm(0, 2)
+        pair(5)
+        grps = e_ctx(t_ctx(1))
+        acc = {}
+        acc[(0, 2)] = mm(0, 2)
         q_ctx(1, grps)
-        fbadd(1)
-        fbadd(2)
-        yadd(0, 2, acc)
-        mean(0)
+        for b in range(1, NB):
+            fbadd(b)
 
-        late = []
-        for b in range(NB):
-            nxt = b + 1
-            nv = NCH - 1 if b in GP_TILES else NCH
+        def square(b):
             nc.scalar.activation(
                 out=sqj[:], in_=y[b][:], func=ACT.Square, bias=negmean[b][:], scale=1.0, accum_out=ssq[b][:]
             )
-            if nxt < NB:
-                acc0 = mm(nxt, 0)
-            t = work.tile([P, H], F32, name="t", tag="t")
-            for n in range(nv):
+            nc.scalar.activation(out=std[b][:], in_=ssq[b][:], func=ACT.Sqrt, bias=eps_t[:], scale=1.0 / H)
+
+        def n_vec(b):
+            return NCH - 1 if b in GP_TILES else NCH
+
+        t_of = {}
+        o_of = {}
+
+        def centre(b):
+            t_of[b] = work.tile([P, H], F32, name="t", tag="t")
+            for n in range(n_vec(b)):
                 sl = slice(n * CH, (n + 1) * CH)
                 nc.vector.scalar_tensor_tensor(
-                    out=t[:, sl], in0=y[b][:, sl], scalar=negmean[b][:], in1=g_ps[n], op0=ALU.add, op1=ALU.mult
+                    out=t_of[b][:, sl], in0=y[b][:, sl], scalar=negmean[b][:], in1=g_ps[n], op0=ALU.add, op1=ALU.mult
                 )
-            nc.scalar.activation(out=std[b][:], in_=ssq[b][:], func=ACT.Sqrt, bias=eps_t[:], scale=1.0 / H)
-            if nxt < NB:
-                acc1 = mm(nxt, 1)
-            if nxt + 1 < NB:
-                grps = t_ctx(nxt + 1)
-            if nxt < NB:
-                yadd(nxt, 0, acc0)
+
+        def recip(b):
             nc.vector.reciprocal(out=rstd[b][:], in_=std[b][:])
-            o = o_pool.tile([P, H], F32, name="o", tag="o")
-            if nv < NCH:
-                sl = slice(nv * CH, (nv + 1) * CH)
-                z1 = zpool.tile([P, CH], F32, name="z1", tag="z1")
-                nc.gpsimd.tensor_scalar(
-                    out=z1[:], in0=y[b][:, sl], scalar1=negmean[b][:], scalar2=rstd[b][:], op0=ALU.add, op1=ALU.mult
+            o_of[b] = o_pool.tile([P, H], F32, name="o", tag="o")
+            if n_vec(b) < NCH:
+                sl = slice((NCH - 1) * CH, H)
+                z1 = work.tile([P, CH], F32, name="z1", tag="z1")
+                nc.scalar.activation(out=nmr[b][:], in_=negmean[b][:], func=ACT.Identity, scale=rstd[b][:])
+                nc.scalar.activation(
+                    out=z1[:], in_=y[b][:, sl], func=ACT.Identity, scale=rstd[b][:], bias=nmr[b][:]
                 )
-                z2 = zpool.tile([P, CH], F32, name="z2", tag="z2")
+                z2 = work.tile([P, CH], F32, name="z2", tag="z2")
                 nc.gpsimd.tensor_tensor(out=z2[:], in0=z1[:], in1=g_sb[:], op=ALU.mult)
-                nc.gpsimd.tensor_tensor(out=o[:, sl], in0=z2[:], in1=b_sb[:], op=ALU.add)
-                fresh = [(b, o)]
-            else:
-                fresh = []
-            if nxt + 2 < NB:
-                fbadd(nxt + 2)
-            for n in range(nv):
+                nc.gpsimd.tensor_tensor(out=o_of[b][:, sl], in0=z2[:], in1=b_sb[:], op=ALU.add)
+
+        def late_finish(b):
+            if b >= 0 and n_vec(b) < NCH:
+                finish(b, (NCH - 1) * CH, H, o_of[b])
+
+        def scale_shift(b, late_b):
+            for n in range(n_vec(b)):
                 halves = 2 if (b == NB - 1 and n == NCH - 1) else 1
                 w = CH // halves
                 for h in range(halves):
                     lo = n * CH + h * w
                     nc.vector.scalar_tensor_tensor(
-                        out=o[:, lo : lo + w], in0=t[:, lo : lo + w], scalar=rstd[b][:],
+                        out=o_of[b][:, lo : lo + w], in0=t_of[b][:, lo : lo + w], scalar=rstd[b][:],
                         in1=b_ps[n][:, h * w : (h + 1) * w], op0=ALU.mult, op1=ALU.add,
                     )
-                    finish(b, lo, lo + w, o)
-                if n == 1:
-                    for item in late:
-                        finish(item[0], (NCH - 1) * CH, H, item[1])
-                    late = []
-            late = late + fresh
-            if nxt < NB:
-                acc2 = mm(nxt, 2)
-                yadd(nxt, 1, acc1)
-                if nxt + 1 < NB:
-                    q_ctx(nxt + 1, grps)
-                yadd(nxt, 2, acc2)
-                mean(nxt)
-        for item in late:
-            finish(item[0], (NCH - 1) * CH, H, item[1])
+                    finish(b, lo, lo + w, o_of[b])
+                if n == LATE_AFTER[b]:
+                    late_finish(late_b)
+
+        acc[(1, 0)] = mm(1, 0)
+        acc[(1, 1)] = mm(1, 1)
+        yadd(0, 2, acc[(0, 2)])
+        mean(0)
+        square(0)
+        acc[(1, 2)] = mm(1, 2)
+        pts = t_ctx(2)
+        centre(0)
+        grps = e_ctx(pts)
+        for p in range(1, NB):
+            yadd(p, 0, acc[(p, 0)])
+            recip(p - 1)
+            yadd(p, 1, acc[(p, 1)])
+            yadd(p, 2, acc[(p, 2)])
+            mean(p)
+            square(p)
+            if p + 1 < NB:
+                q_ctx(p + 1, grps)
+                for n in range(NCH):
+                    acc[(p + 1, n)] = mm(p + 1, n)
+            if p + 2 < NB:
+                pts = t_ctx(p + 2)
+            scale_shift(p - 1, p - 2)
+            centre(p)
+            if p + 2 < NB:
+                grps = e_ctx(pts)
+        recip(NB - 1)
+        scale_shift(NB - 1, NB - 2)

from contextlib import ExitStack

import concourse.mybir as mybir
from concourse.masks import make_identity

FLOPS = 2 * 512 * 1536 * 1536

F32 = mybir.dt.float32
BF16 = mybir.dt.bfloat16
U32 = mybir.dt.uint32
U8 = mybir.dt.uint8
FP8X4 = mybir.dt.float8_e4m3fn_x4
FP8 = mybir.dt.float8_e4m3fn
ALU = mybir.AluOpType
ACT = mybir.ActivationFunctionType

P = 128
NB = 4
NH = 12
K = 1536
H = 1536
NPASS = 3
CH = 512
NCH = 3
LN_EPS = 1e-5
Y_SCALE = 210.0

GP_TILES = [0,1,2]
LATE_AFTER = [1, 1, 1, 1]
N_WARM = 4
GP_FB = [1,2,3]


def tile_hierarchicalattention_pb_kernel(tc, ctx_heads, Wo, bo, features, ln_g, ln_b, out_0, out_1):
    nc = tc.nc
    with ExitStack() as es:
        keep = es.enter_context(tc.tile_pool(name="keep", bufs=1))
        grp_pool = es.enter_context(tc.tile_pool(name="grp", bufs=6))
        work = es.enter_context(tc.tile_pool(name="work", bufs=2))
        o_pool = es.enter_context(tc.tile_pool(name="op", bufs=3))
        o8_pool = es.enter_context(tc.tile_pool(name="o8p", bufs=6))
        ps = es.enter_context(tc.psum_pool(name="ps", bufs=5))
        psk = es.enter_context(tc.psum_pool(name="psk", bufs=1))
        es.enter_context(tc.manual_schedule())

        x_sb = [keep.tile([P, K], BF16, name="x%d" % b) for b in range(NB)]
        wp = [keep.tile([P, 2, K], BF16, name="wp%d" % i) for i in range(6)]
        f_sb = [keep.tile([P, H], BF16, name="f%d" % b) for b in range(NB)]
        fb = [keep.tile([P, H], F32, name="fb%d" % b) for b in range(NB)]
        y = [keep.tile([P, H], F32, name="y%d" % b) for b in range(NB)]
        xq = [keep.tile([P, NPASS * P], U32, name="xq%d" % b, align_bytes=64) for b in range(NB)]
        xs = [keep.tile([P, NPASS * P], U8, name="xs%d" % b, align_bytes=64) for b in range(NB)]
        wq = keep.tile([P, NPASS, H], U32, name="wq", align_bytes=64)
        ws = keep.tile([P, NPASS, H], U8, name="ws", align_bytes=64)
        vbo = keep.tile([P, H], BF16, name="vbo")
        vgb = keep.tile([P, H], BF16, name="vgb")
        bo_b = keep.tile([P, H], BF16, name="bo_b")
        g_sb = keep.tile([P, CH], BF16, name="g_sb")
        b_sb = keep.tile([P, CH], BF16, name="b_sb")
        zeros = keep.tile([P, CH], BF16, name="zeros")
        ident_f = keep.tile([P, P], F32, name="ident_f")
        ident_b = keep.tile([P, P], BF16, name="ident_b")
        eps_t = keep.tile([P, 1], F32, name="eps_t")
        warm = keep.tile([P, 1], F32, name="warm")
        sqj = keep.tile([P, H], F32, name="sqj")
        sums = [keep.tile([P, NCH], F32, name="sums%d" % b) for b in range(NB)]
        junk3 = [keep.tile([P, NCH], F32, name="junk3%d" % b) for b in range(NB)]
        negmean = [keep.tile([P, 1], F32, name="negmean%d" % b) for b in range(NB)]
        ssq = [keep.tile([P, 1], F32, name="ssq%d" % b) for b in range(NB)]
        std = [keep.tile([P, 1], F32, name="std%d" % b) for b in range(NB)]
        rstd = [keep.tile([P, 1], F32, name="rstd%d" % b) for b in range(NB)]
        nmr = [keep.tile([P, 1], F32, name="nmr%d" % b) for b in range(NB)]
        gb = [psk.tile([P, 1024], BF16, name="gb%d" % i) for i in range(3)]
        g_ps = [gb[0][:, 0:512], gb[0][:, 512:1024], gb[1][:, 0:512]]
        b_ps = [gb[1][:, 512:1024], gb[2][:, 0:512], gb[2][:, 512:1024]]

        nc.vector.memset(zeros[:], 0.0)
        nc.vector.memset(vbo[:], 0.0)
        nc.vector.memset(eps_t[:], LN_EPS)
        make_identity(nc, ident_b[:])
        nc.gpsimd.memset(vgb[:], 0.0)
        make_identity(nc, ident_f[:])
        nc.scalar.activation(out=warm[:], in_=eps_t[:], func=ACT.Sqrt)

        def load_ctx(b):
            nc.sync.dma_start(
                out=x_sb[b][:].rearrange("p (h d) -> p h d", h=NH),
                in_=ctx_heads[b].rearrange("h s d -> s h d"),
            )

        def load_pair(i):
            nc.sync.dma_start(out=wp[i][:], in_=Wo[2 * i * P : (2 * i + 2) * P, :].rearrange("(a p) k -> p a k", a=2))

        def load_f(b):
            nc.sync.dma_start(out=f_sb[b][:], in_=features[b])

        load_ctx(0)
        nc.sync.dma_start(out=vbo[0:1, :], in_=bo.rearrange("(o n) -> o n", o=1))
        nc.sync.dma_start(out=wp[0][:, 0, :], in_=Wo[0:P, :])
        nc.sync.dma_start(out=wp[0][:, 1, :], in_=Wo[P : 2 * P, :])
        nc.sync.dma_start(out=vgb[0:1, :], in_=ln_g.rearrange("(o n) -> o n", o=1))
        nc.sync.dma_start(out=vgb[1:2, :], in_=ln_b.rearrange("(o n) -> o n", o=1))
        load_pair(1)
        load_f(0)
        load_pair(2)
        load_pair(3)
        load_pair(4)
        for g in range(NPASS):
            nc.sync.dma_start(
                out=wp[5][:, :, g * 512 : (g + 1) * 512],
                in_=Wo[10 * P : 12 * P, g * 512 : (g + 1) * 512].rearrange("(a p) k -> p a k", a=2),
            )
        for b in range(1, NB):
            load_ctx(b)
            load_f(b)

        def transpose_words(dst, src, g, u):
            words = src.bitcast(F32)
            nc.tensor.transpose(dst, words[:, 256 * g + u : 256 * (g + 1) : 2], ident_f[:])

        def evacuate(pt, ncol):
            grp = grp_pool.tile([P, 1024], BF16, name="grp", tag="grp", align_bytes=64)
            a = ncol // 256
            nc.scalar.copy(
                out=grp[:, 0 : 2 * ncol].bitcast(F32).rearrange("p (a r u) -> p a r u", a=a, u=2),
                in_=pt[:, 0:ncol].rearrange("p (a u r) -> p a r u", a=a, u=2),
            )
            return grp

        def t_ctx(b):
            pa = ps.tile([P, CH], F32, name="wk", tag="wk")
            for g in range(2):
                for u in range(2):
                    transpose_words(pa[:, (2 * g + u) * P : (2 * g + u + 1) * P], x_sb[b][:], g, u)
            pb = ps.tile([P, CH], F32, name="wk", tag="wk")
            for u in range(2):
                transpose_words(pb[:, u * P : (u + 1) * P], x_sb[b][:], 2, u)
            return pa, pb

        def e_ctx(pts):
            return evacuate(pts[0], 512), evacuate(pts[1], 256)

        def q_ctx(b, grps):
            nc.vector.quantize_mx(out=xq[b][:, 0:256].bitcast(FP8X4), scales=xs[b][:, 0:256], in_=grps[0][:])
            nc.vector.quantize_mx(
                out=xq[b][:, 256:384].bitcast(FP8X4), scales=xs[b][:, 256:384], in_=grps[1][:, 0:512]
            )

        def pair(i):
            grps = []
            for g in range(NPASS):
                pt = ps.tile([P, CH], F32, name="wk", tag="wk")
                for a in range(2):
                    for u in range(2):
                        transpose_words(pt[:, (2 * a + u) * P : (2 * a + u + 1) * P], wp[i][:, a, :], g, u)
                grps.append(evacuate(pt, 512))
            for g in range(NPASS):
                cols = slice(256 * i, 256 * (i + 1))
                nc.vector.quantize_mx(out=wq[:, g, cols].bitcast(FP8X4), scales=ws[:, g, cols], in_=grps[g][:])

        def bcast(src, j, n, dst):
            nc.tensor.matmul(
                out=dst,
                lhsT=ident_b[:, j : j + 1].to_broadcast([P, P]),
                rhs=src[:, n * CH : (n + 1) * CH],
                start=True,
                stop=True,
            )

        def mm(b, n):
            acc = ps.tile([P, CH], F32, name="wk", tag="wk")
            for g in range(NPASS):
                nc.tensor.matmul_mx(
                    out=acc[:],
                    lhsT=xq[b][:, g * P : (g + 1) * P].bitcast(FP8X4),
                    lhsT_scale=xs[b][:, g * P : (g + 1) * P],
                    rhs=wq[:, g, n * CH : (n + 1) * CH].bitcast(FP8X4),
                    rhs_scale=ws[:, g, n * CH : (n + 1) * CH],
                    start=(g == 0),
                    stop=(g == NPASS - 1),
                )
            return acc

        def fbadd(b):
            if b in GP_FB:
                for n in range(NCH):
                    sl = slice(n * CH, (n + 1) * CH)
                    nc.gpsimd.tensor_tensor(out=fb[b][:, sl], in0=f_sb[b][:, sl], in1=bo_b[:, sl], op=ALU.add)
            else:
                nc.vector.tensor_tensor(out=fb[b][:], in0=f_sb[b][:], in1=bo_b[:], op=ALU.add)

        def yadd(b, n, acc):
            sl = slice(n * CH, (n + 1) * CH)
            nc.vector.scalar_tensor_tensor(
                out=y[b][:, sl], in0=acc[:], scalar=1.0, in1=fb[b][:, sl],
                op0=ALU.mult, op1=ALU.add, accum_out=sums[b][:, n : n + 1],
            )

        def mean(b):
            nc.vector.tensor_scalar(
                out=junk3[b][:], in0=sums[b][:], scalar1=-1.0 / H, scalar2=None,
                op0=ALU.mult, op1=ALU.add, accum_out=negmean[b][:],
            )

        def finish(b, lo, hi, o):
            nc.sync.dma_start(out=out_0[b, :, lo:hi], in_=o[:, lo:hi])
            o8 = o8_pool.tile([P, CH], FP8, name="o8", tag="o8")
            nc.scalar.activation(
                out=o8[:, 0 : hi - lo], in_=o[:, lo:hi], func=ACT.Copy, scale=Y_SCALE, saturate=False
            )
            nc.sync.dma_start(out=out_1[b, :, lo:hi], in_=o8[:, 0 : hi - lo].bitcast(U8))

        dummy = ps.tile([P, CH], F32, name="wk", tag="wk")
        for i in range(N_WARM):
            nc.tensor.matmul(out=dummy[:], lhsT=ident_b[:], rhs=zeros[:], start=True, stop=True)
        grps = e_ctx(t_ctx(0))
        bca = ps.tile([P, 1024], BF16, name="wk", tag="wk")
        bcast(vbo, 0, 0, bca[:, 0:512])
        bcast(vbo, 0, 1, bca[:, 512:1024])
        nc.scalar.copy(out=bo_b[:, 0:1024], in_=bca[:])
        q_ctx(0, grps)
        pair(0)
        bcb = ps.tile([P, 1024], BF16, name="wk", tag="wk")
        bcast(vbo, 0, 2, bcb[:, 0:512])
        bcast(vgb, 0, 0, g_ps[0])
        nc.scalar.copy(out=bo_b[:, 1024:1536], in_=bcb[:, 0:512])
        pair(1)
        bcast(vgb, 0, 1, g_ps[1])
        bcast(vgb, 0, 2, g_ps[2])
        pair(2)
        for n in range(NCH):
            bcast(vgb, 1, n, b_ps[n])
        fbadd(0)
        pair(3)
        if GP_TILES:
            nc.scalar.copy(out=g_sb[:], in_=g_ps[2])
            nc.scalar.copy(out=b_sb[:], in_=b_ps[2])
        yadd(0, 0, mm(0, 0))
        pair(4)
        yadd(0, 1, mm(0, 1))
        pair(5)
        grps = e_ctx(t_ctx(1))
        acc = {}
        acc[(0, 2)] = mm(0, 2)
        q_ctx(1, grps)
        for b in range(1, NB):
            fbadd(b)

        def square(b):
            nc.scalar.activation(
                out=sqj[:], in_=y[b][:], func=ACT.Square, bias=negmean[b][:], scale=1.0, accum_out=ssq[b][:]
            )
            nc.scalar.activation(out=std[b][:], in_=ssq[b][:], func=ACT.Sqrt, bias=eps_t[:], scale=1.0 / H)

        def n_vec(b):
            return NCH - 1 if b in GP_TILES else NCH

        t_of = {}
        o_of = {}

        def centre(b):
            t_of[b] = work.tile([P, H], F32, name="t", tag="t")
            for n in range(n_vec(b)):
                sl = slice(n * CH, (n + 1) * CH)
                nc.vector.scalar_tensor_tensor(
                    out=t_of[b][:, sl], in0=y[b][:, sl], scalar=negmean[b][:], in1=g_ps[n], op0=ALU.add, op1=ALU.mult
                )

        def recip(b):
            nc.vector.reciprocal(out=rstd[b][:], in_=std[b][:])
            o_of[b] = o_pool.tile([P, H], F32, name="o", tag="o")
            if n_vec(b) < NCH:
                sl = slice((NCH - 1) * CH, H)
                z1 = work.tile([P, CH], F32, name="z1", tag="z1")
                nc.scalar.activation(out=nmr[b][:], in_=negmean[b][:], func=ACT.Identity, scale=rstd[b][:])
                nc.scalar.activation(
                    out=z1[:], in_=y[b][:, sl], func=ACT.Identity, scale=rstd[b][:], bias=nmr[b][:]
                )
                z2 = work.tile([P, CH], F32, name="z2", tag="z2")
                nc.gpsimd.tensor_tensor(out=z2[:], in0=z1[:], in1=g_sb[:], op=ALU.mult)
                nc.gpsimd.tensor_tensor(out=o_of[b][:, sl], in0=z2[:], in1=b_sb[:], op=ALU.add)

        def late_finish(b):
            if b >= 0 and n_vec(b) < NCH:
                finish(b, (NCH - 1) * CH, H, o_of[b])

        def scale_shift(b, late_b):
            for n in range(n_vec(b)):
                halves = 2 if (b == NB - 1 and n == NCH - 1) else 1
                w = CH // halves
                for h in range(halves):
                    lo = n * CH + h * w
                    nc.vector.scalar_tensor_tensor(
                        out=o_of[b][:, lo : lo + w], in0=t_of[b][:, lo : lo + w], scalar=rstd[b][:],
                        in1=b_ps[n][:, h * w : (h + 1) * w], op0=ALU.mult, op1=ALU.add,
                    )
                    finish(b, lo, lo + w, o_of[b])
                if n == LATE_AFTER[b]:
                    late_finish(late_b)

        acc[(1, 0)] = mm(1, 0)
        acc[(1, 1)] = mm(1, 1)
        yadd(0, 2, acc[(0, 2)])
        mean(0)
        square(0)
        acc[(1, 2)] = mm(1, 2)
        pts = t_ctx(2)
        centre(0)
        grps = e_ctx(pts)
        for p in range(1, NB):
            yadd(p, 0, acc[(p, 0)])
            recip(p - 1)
            yadd(p, 1, acc[(p, 1)])
            yadd(p, 2, acc[(p, 2)])
            mean(p)
            square(p)
            if p + 1 < NB:
                q_ctx(p + 1, grps)
                for n in range(NCH):
                    acc[(p + 1, n)] = mm(p + 1, n)
            if p + 2 < NB:
                pts = t_ctx(p + 2)
            scale_shift(p - 1, p - 2)
            centre(p)
            if p + 2 < NB:
                grps = e_ctx(pts)
        recip(NB - 1)
        scale_shift(NB - 1, NB - 2)
